import numpy as np
import ml_dtypes

BF16 = ml_dtypes.bfloat16


def bf(x):
    return np.asarray(x, np.float32).astype(BF16)


def f32(x):
    return np.asarray(x, np.float32)


def f64(x):
    return np.asarray(x).astype(np.float64)


def striped(idx):
    return np.tile(idx.reshape(-1, 16).T, (8, 1))


B, T, CH, KP, SM, P, STRETCH, S, N, H, R = 128, 256, 8, 32, 32, 8, 8, 2048, 8192, 1024, 8
SLOPE = 0.3


def setup_inputs():
    x = f32(np.random.standard_normal((B, S)))
    w = f32(np.random.standard_normal((1, N)) / np.sqrt(KP))
    b = f32(0.1 * np.random.standard_normal((1, SM * P)))
    idx = np.concatenate([np.random.permutation(S)[:H] for _ in range(R)])
    return {"x": x, "w": w, "b": b, "offs": striped(idx)}


def reference(x, w, b, offs):
    idx = offs[:16].T.reshape(-1)
    prod = f64(x)[:, idx] * f64(w)
    v = prod.reshape(B, SM, P, KP).sum(axis=-1) + f64(b).reshape(1, SM, P)
    a = np.maximum(v, SLOPE * v)
    return np.repeat(a, STRETCH, axis=1).reshape(B, T * P)

@@ -1,0 +1,70 @@
+import concourse.mybir as mybir
+
+F32 = mybir.dt.float32
+U16 = mybir.dt.uint16
+ALU = mybir.AluOpType
+AXIS = mybir.AxisListType
+
+SAMPLES = 128
+POINTS = 2048
+ENTRIES = 8192
+PLACES = 32
+PER_STEP = 8
+STRETCH = 8
+SLOPE = 0.3
+
+PIECE = 1024
+PIECES = ENTRIES // PIECE
+PIECE_PATCHES = PIECE // PLACES
+PIECE_STEPS = PIECE_PATCHES // PER_STEP
+PIECE_OUT = PIECE_PATCHES * STRETCH
+
+FLOPS = 2 * SAMPLES * ENTRIES
+
+
+def tile_patchy_layer_returnfullseq_kernel(tc, x, w, b, offs, out):
+    nc = tc.nc
+    with (
+        tc.tile_pool(name="held", bufs=1) as held,
+        tc.tile_pool(name="ring", bufs=2) as ring,
+    ):
+        offsets = held.tile([SAMPLES, ENTRIES // 16], U16, name="offsets")
+        nc.sync.dma_start(offsets[:], offs)
+        window = held.tile([SAMPLES, POINTS], F32, name="window")
+        nc.sync.dma_start(window[:], x)
+        bias = held.tile([SAMPLES, ENTRIES // PLACES], F32, name="bias")
+        nc.sync.dma_start(bias[:], b.broadcast_to([SAMPLES, ENTRIES // PLACES]))
+
+        for k in range(PIECES):
+            weights = ring.tile([SAMPLES, PIECE], F32, name="weights")
+            nc.sync.dma_start(
+                weights[:], w[:, k * PIECE : (k + 1) * PIECE].broadcast_to([SAMPLES, PIECE])
+            )
+
+            product = ring.tile([SAMPLES, PIECE], F32, name="product")
+            picked = window[:].indirect(offsets[:, k * (PIECE // 16) : (k + 1) * (PIECE // 16)])
+            nc.vector.tensor_tensor(product[:], picked, weights[:], ALU.mult)
+
+            sums = ring.tile([SAMPLES, PIECE_PATCHES], F32, name="sums")
+            nc.vector.tensor_reduce(
+                sums[:], product[:].rearrange("c (q i) -> c q i", i=PLACES), AXIS.X, ALU.add
+            )
+            nc.vector.tensor_tensor(
+                sums[:], sums[:], bias[:, k * PIECE_PATCHES : (k + 1) * PIECE_PATCHES], ALU.add
+            )
+
+            active = ring.tile([SAMPLES, PIECE_PATCHES], F32, name="active")
+            nc.vector.scalar_tensor_tensor(active[:], sums[:], SLOPE, sums[:], ALU.mult, ALU.max)
+
+            stretched = ring.tile([SAMPLES, PIECE_STEPS, STRETCH, PER_STEP], F32, name="stretched")
+            nc.vector.tensor_copy(
+                stretched[:],
+                active[:]
+                .rearrange("c (s p) -> c s p", p=PER_STEP)
+                .unsqueeze(2)
+                .broadcast_to([SAMPLES, PIECE_STEPS, STRETCH, PER_STEP]),
+            )
+            nc.sync.dma_start(
+                out[:, k * PIECE_OUT : (k + 1) * PIECE_OUT],
+                stretched[:].rearrange("c s r p -> c (s r p)"),
+            )

@@ -1,14 +1,16 @@
 import concourse.mybir as mybir
+from concourse.masks import make_identity
 
 F32 = mybir.dt.float32
 U16 = mybir.dt.uint16
 ALU = mybir.AluOpType
-AXIS = mybir.AxisListType
+FUNC = mybir.ActivationFunctionType
 
 SAMPLES = 128
 POINTS = 2048
 ENTRIES = 8192
 PLACES = 32
+PATCHES = ENTRIES // PLACES
 PER_STEP = 8
 STRETCH = 8
 SLOPE = 0.3
@@ -19,6 +21,10 @@ PIECE_PATCHES = PIECE // PLACES
 PIECE_STEPS = PIECE_PATCHES // PER_STEP
 PIECE_OUT = PIECE_PATCHES * STRETCH
 
+RUNS = 128
+RUN = PIECE // RUNS
+PATCH_RUNS = PLACES // RUN
+
 FLOPS = 2 * SAMPLES * ENTRIES
 
 
@@ -26,43 +32,89 @@ def tile_patchy_layer_returnfullseq_kernel(tc, x, w, b, offs, out):
     nc = tc.nc
     with (
         tc.tile_pool(name="held", bufs=1) as held,
-        tc.tile_pool(name="ring", bufs=2) as ring,
+        tc.tile_pool(name="ring", bufs=3) as ring,
+        tc.psum_pool(name="psum", bufs=2) as psum,
     ):
         offsets = held.tile([SAMPLES, ENTRIES // 16], U16, name="offsets")
         nc.sync.dma_start(offsets[:], offs)
         window = held.tile([SAMPLES, POINTS], F32, name="window")
         nc.sync.dma_start(window[:], x)
-        bias = held.tile([SAMPLES, ENTRIES // PLACES], F32, name="bias")
-        nc.sync.dma_start(bias[:], b.broadcast_to([SAMPLES, ENTRIES // PLACES]))
+        weights = [held.tile([SAMPLES, PIECE], F32, name=f"weights{k}") for k in range(PIECES)]
+        for k in range(PIECES):
+            nc.sync.dma_start(
+                weights[k][:], w[:, k * PIECE : (k + 1) * PIECE].broadcast_to([SAMPLES, PIECE])
+            )
+        bias_row = held.tile([1, PATCHES], F32, name="bias_row")
+        nc.sync.dma_start(bias_row[:], b)
+
+        identity = held.tile([SAMPLES, SAMPLES], F32, name="identity")
+        make_identity(nc, identity[:])
+        ones_row = held.tile([1, SAMPLES], F32, name="ones_row")
+        nc.gpsimd.memset(ones_row[:], 1.0)
+        run_of_patch = held.tile([RUNS, PIECE_PATCHES], F32, name="run_of_patch")
+        nc.gpsimd.memset(run_of_patch[:], 1.0)
+        nc.gpsimd.affine_select(
+            out=run_of_patch[:],
+            in_=run_of_patch[:],
+            pattern=[[-PATCH_RUNS, PIECE_PATCHES]],
+            compare_op=ALU.is_ge,
+            fill=0.0,
+            base=0,
+            channel_multiplier=1,
+        )
+        nc.gpsimd.affine_select(
+            out=run_of_patch[:],
+            in_=run_of_patch[:],
+            pattern=[[PATCH_RUNS, PIECE_PATCHES]],
+            compare_op=ALU.is_ge,
+            fill=0.0,
+            base=PATCH_RUNS - 1,
+            channel_multiplier=-1,
+        )
 
         for k in range(PIECES):
-            weights = ring.tile([SAMPLES, PIECE], F32, name="weights")
-            nc.sync.dma_start(
-                weights[:], w[:, k * PIECE : (k + 1) * PIECE].broadcast_to([SAMPLES, PIECE])
-            )
-
             product = ring.tile([SAMPLES, PIECE], F32, name="product")
             picked = window[:].indirect(offsets[:, k * (PIECE // 16) : (k + 1) * (PIECE // 16)])
-            nc.vector.tensor_tensor(product[:], picked, weights[:], ALU.mult)
+            nc.vector.tensor_tensor(product[:], picked, weights[k][:], ALU.mult)
 
-            sums = ring.tile([SAMPLES, PIECE_PATCHES], F32, name="sums")
-            nc.vector.tensor_reduce(
-                sums[:], product[:].rearrange("c (q i) -> c q i", i=PLACES), AXIS.X, ALU.add
+            by_run = product[:].rearrange("c (m j) -> c m j", j=RUN)
+            run_sums_psum = psum.tile([RUNS, SAMPLES], F32, name="run_sums_psum")
+            for j in range(RUN):
+                nc.tensor.matmul(
+                    run_sums_psum[:],
+                    lhsT=by_run[:, :, j],
+                    rhs=identity[:],
+                    start=(j == 0),
+                    stop=(j == RUN - 1),
+                    is_transpose=True,
+                )
+            run_sums = ring.tile([RUNS, SAMPLES], F32, name="run_sums")
+            nc.scalar.activation(run_sums[:], run_sums_psum[:], FUNC.Copy)
+
+            v_psum = psum.tile([SAMPLES, PIECE_PATCHES], F32, name="v_psum")
+            nc.tensor.matmul(
+                v_psum[:],
+                lhsT=ones_row[:],
+                rhs=bias_row[:, k * PIECE_PATCHES : (k + 1) * PIECE_PATCHES],
+                start=True,
+                stop=False,
             )
-            nc.vector.tensor_tensor(
-                sums[:], sums[:], bias[:, k * PIECE_PATCHES : (k + 1) * PIECE_PATCHES], ALU.add
+            nc.tensor.matmul(v_psum[:], lhsT=run_sums[:], rhs=run_of_patch[:], start=False, stop=True)
+
+            sloped = ring.tile([SAMPLES, PIECE_STEPS, 1, PER_STEP], F32, name="sloped")
+            nc.scalar.activation(
+                sloped[:].rearrange("c s r p -> c (s r p)"), v_psum[:], FUNC.Copy, scale=SLOPE
             )
-
-            active = ring.tile([SAMPLES, PIECE_PATCHES], F32, name="active")
-            nc.vector.scalar_tensor_tensor(active[:], sums[:], SLOPE, sums[:], ALU.mult, ALU.max)
-
+            lifted = ring.tile([SAMPLES, PIECE_STEPS, 1, PER_STEP], F32, name="lifted")
+            nc.scalar.activation(
+                lifted[:].rearrange("c s r p -> c (s r p)"), v_psum[:], FUNC.Relu, scale=1.0 - SLOPE
+            )
             stretched = ring.tile([SAMPLES, PIECE_STEPS, STRETCH, PER_STEP], F32, name="stretched")
-            nc.vector.tensor_copy(
+            nc.gpsimd.tensor_tensor(
                 stretched[:],
-                active[:]
-                .rearrange("c (s p) -> c s p", p=PER_STEP)
-                .unsqueeze(2)
-                .broadcast_to([SAMPLES, PIECE_STEPS, STRETCH, PER_STEP]),
+                sloped[:].broadcast_to([SAMPLES, PIECE_STEPS, STRETCH, PER_STEP]),
+                lifted[:].broadcast_to([SAMPLES, PIECE_STEPS, STRETCH, PER_STEP]),
+                ALU.add,
             )
             nc.sync.dma_start(
                 out[:, k * PIECE_OUT : (k + 1) * PIECE_OUT],

@@ -101,20 +101,18 @@ def tile_patchy_layer_returnfullseq_kernel(tc, x, w, b, offs, out):
             )
             nc.tensor.matmul(v_psum[:], lhsT=run_sums[:], rhs=run_of_patch[:], start=False, stop=True)
 
-            sloped = ring.tile([SAMPLES, PIECE_STEPS, 1, PER_STEP], F32, name="sloped")
-            nc.scalar.activation(
-                sloped[:].rearrange("c s r p -> c (s r p)"), v_psum[:], FUNC.Copy, scale=SLOPE
+            sloped = ring.tile([SAMPLES, PIECE_PATCHES], F32, name="sloped")
+            nc.scalar.activation(sloped[:], v_psum[:], FUNC.Copy, scale=SLOPE)
+            active = ring.tile([SAMPLES, PIECE_STEPS, 1, PER_STEP], F32, name="active")
+            nc.vector.tensor_tensor(
+                active[:].rearrange("c s r p -> c (s r p)"), v_psum[:], sloped[:], ALU.max
             )
-            lifted = ring.tile([SAMPLES, PIECE_STEPS, 1, PER_STEP], F32, name="lifted")
-            nc.scalar.activation(
-                lifted[:].rearrange("c s r p -> c (s r p)"), v_psum[:], FUNC.Relu, scale=1.0 - SLOPE
-            )
+
             stretched = ring.tile([SAMPLES, PIECE_STEPS, STRETCH, PER_STEP], F32, name="stretched")
-            nc.gpsimd.tensor_tensor(
+            nc.scalar.activation(
                 stretched[:],
-                sloped[:].broadcast_to([SAMPLES, PIECE_STEPS, STRETCH, PER_STEP]),
-                lifted[:].broadcast_to([SAMPLES, PIECE_STEPS, STRETCH, PER_STEP]),
-                ALU.add,
+                active[:].broadcast_to([SAMPLES, PIECE_STEPS, STRETCH, PER_STEP]),
+                FUNC.Copy,
             )
             nc.sync.dma_start(
                 out[:, k * PIECE_OUT : (k + 1) * PIECE_OUT],

@@ -4,6 +4,7 @@ from concourse.masks import make_identity
 F32 = mybir.dt.float32
 U16 = mybir.dt.uint16
 ALU = mybir.AluOpType
+AXIS = mybir.AxisListType
 FUNC = mybir.ActivationFunctionType
 
 SAMPLES = 128
@@ -25,6 +26,8 @@ RUNS = 128
 RUN = PIECE // RUNS
 PATCH_RUNS = PLACES // RUN
 
+LAG = 3
+
 FLOPS = 2 * SAMPLES * ENTRIES
 
 
@@ -32,25 +35,25 @@ def tile_patchy_layer_returnfullseq_kernel(tc, x, w, b, offs, out):
     nc = tc.nc
     with (
         tc.tile_pool(name="held", bufs=1) as held,
-        tc.tile_pool(name="ring", bufs=3) as ring,
+        tc.tile_pool(name="ring", bufs=LAG + 2) as ring,
         tc.psum_pool(name="psum", bufs=2) as psum,
+        tc.psum_pool(name="psum_waiting", bufs=LAG + 2) as psum_waiting,
     ):
         offsets = held.tile([SAMPLES, ENTRIES // 16], U16, name="offsets")
         nc.sync.dma_start(offsets[:], offs)
         window = held.tile([SAMPLES, POINTS], F32, name="window")
         nc.sync.dma_start(window[:], x)
         weights = [held.tile([SAMPLES, PIECE], F32, name=f"weights{k}") for k in range(PIECES)]
+        bias = held.tile([SAMPLES, PATCHES], F32, name="bias")
         for k in range(PIECES):
             nc.sync.dma_start(
                 weights[k][:], w[:, k * PIECE : (k + 1) * PIECE].broadcast_to([SAMPLES, PIECE])
             )
-        bias_row = held.tile([1, PATCHES], F32, name="bias_row")
-        nc.sync.dma_start(bias_row[:], b)
+            if k == LAG:
+                nc.sync.dma_start(bias[:], b.broadcast_to([SAMPLES, PATCHES]))
 
         identity = held.tile([SAMPLES, SAMPLES], F32, name="identity")
         make_identity(nc, identity[:])
-        ones_row = held.tile([1, SAMPLES], F32, name="ones_row")
-        nc.gpsimd.memset(ones_row[:], 1.0)
         run_of_patch = held.tile([RUNS, PIECE_PATCHES], F32, name="run_of_patch")
         nc.gpsimd.memset(run_of_patch[:], 1.0)
         nc.gpsimd.affine_select(
@@ -72,12 +75,18 @@ def tile_patchy_layer_returnfullseq_kernel(tc, x, w, b, offs, out):
             channel_multiplier=-1,
         )
 
-        for k in range(PIECES):
-            product = ring.tile([SAMPLES, PIECE], F32, name="product")
-            picked = window[:].indirect(offsets[:, k * (PIECE // 16) : (k + 1) * (PIECE // 16)])
-            nc.vector.tensor_tensor(product[:], picked, weights[k][:], ALU.mult)
+        product = {}
+        sums = {}
 
-            by_run = product[:].rearrange("c (m j) -> c m j", j=RUN)
+        def look_up(k):
+            product[k] = ring.tile([SAMPLES, PIECE], F32, name="product")
+            picked = window[:].indirect(offsets[:, k * (PIECE // 16) : (k + 1) * (PIECE // 16)])
+            nc.vector.tensor_tensor(product[k][:], picked, weights[k][:], ALU.mult)
+
+        run_sums = {}
+
+        def sum_runs(k):
+            by_run = product[k][:].rearrange("c (m j) -> c m j", j=RUN)
             run_sums_psum = psum.tile([RUNS, SAMPLES], F32, name="run_sums_psum")
             for j in range(RUN):
                 nc.tensor.matmul(
@@ -88,26 +97,30 @@ def tile_patchy_layer_returnfullseq_kernel(tc, x, w, b, offs, out):
                     stop=(j == RUN - 1),
                     is_transpose=True,
                 )
-            run_sums = ring.tile([RUNS, SAMPLES], F32, name="run_sums")
-            nc.scalar.activation(run_sums[:], run_sums_psum[:], FUNC.Copy)
+            run_sums[k] = ring.tile([RUNS, SAMPLES], F32, name="run_sums")
+            nc.scalar.activation(run_sums[k][:], run_sums_psum[:], FUNC.Copy)
 
-            v_psum = psum.tile([SAMPLES, PIECE_PATCHES], F32, name="v_psum")
+        def sum_patches(k):
+            sums[k] = psum_waiting.tile([SAMPLES, PIECE_PATCHES], F32, name="sums_psum")
             nc.tensor.matmul(
-                v_psum[:],
-                lhsT=ones_row[:],
-                rhs=bias_row[:, k * PIECE_PATCHES : (k + 1) * PIECE_PATCHES],
-                start=True,
-                stop=False,
+                sums[k][:], lhsT=run_sums[k][:], rhs=run_of_patch[:], start=True, stop=True
             )
-            nc.tensor.matmul(v_psum[:], lhsT=run_sums[:], rhs=run_of_patch[:], start=False, stop=True)
 
-            sloped = ring.tile([SAMPLES, PIECE_PATCHES], F32, name="sloped")
-            nc.scalar.activation(sloped[:], v_psum[:], FUNC.Copy, scale=SLOPE)
-            active = ring.tile([SAMPLES, PIECE_STEPS, 1, PER_STEP], F32, name="active")
+        def sum_on_vector(k):
+            sums[k] = ring.tile([SAMPLES, PIECE_PATCHES], F32, name="sums_sbuf")
+            nc.vector.tensor_reduce(
+                sums[k][:], product[k][:].rearrange("c (q i) -> c q i", i=PLACES), AXIS.X, ALU.add
+            )
+
+        def finish(k):
+            v = ring.tile([SAMPLES, PIECE_PATCHES], F32, name="v")
             nc.vector.tensor_tensor(
-                active[:].rearrange("c s r p -> c (s r p)"), v_psum[:], sloped[:], ALU.max
+                v[:], sums[k][:], bias[:, k * PIECE_PATCHES : (k + 1) * PIECE_PATCHES], ALU.add
             )
-
+            active = ring.tile([SAMPLES, PIECE_STEPS, 1, PER_STEP], F32, name="active")
+            nc.vector.scalar_tensor_tensor(
+                active[:].rearrange("c s r p -> c (s r p)"), v[:], SLOPE, v[:], ALU.mult, ALU.max
+            )
             stretched = ring.tile([SAMPLES, PIECE_STEPS, STRETCH, PER_STEP], F32, name="stretched")
             nc.scalar.activation(
                 stretched[:],
@@ -118,3 +131,16 @@ def tile_patchy_layer_returnfullseq_kernel(tc, x, w, b, offs, out):
                 out[:, k * PIECE_OUT : (k + 1) * PIECE_OUT],
                 stretched[:].rearrange("c s r p -> c (s r p)"),
             )
+
+        last = PIECES - 1
+        for k in range(PIECES):
+            look_up(k)
+            if k >= LAG:
+                finish(k - LAG)
+            if k < last:
+                sum_runs(k)
+            if k >= 1:
+                sum_patches(k - 1)
+        sum_on_vector(last)
+        for k in range(PIECES - LAG, PIECES):
+            finish(k)

@@ -26,9 +26,14 @@ RUNS = 128
 RUN = PIECE // RUNS
 PATCH_RUNS = PLACES // RUN
 
+HEAD = 256
 LAG = 3
 
 FLOPS = 2 * SAMPLES * ENTRIES
+
+
+def parts_of(k):
+    return ((0, HEAD), (HEAD, PIECE)) if k == 0 else ((0, PIECE),)
 
 
 def tile_patchy_layer_returnfullseq_kernel(tc, x, w, b, offs, out):
@@ -46,9 +51,11 @@ def tile_patchy_layer_returnfullseq_kernel(tc, x, w, b, offs, out):
         weights = [held.tile([SAMPLES, PIECE], F32, name=f"weights{k}") for k in range(PIECES)]
         bias = held.tile([SAMPLES, PATCHES], F32, name="bias")
         for k in range(PIECES):
-            nc.sync.dma_start(
-                weights[k][:], w[:, k * PIECE : (k + 1) * PIECE].broadcast_to([SAMPLES, PIECE])
-            )
+            for lo, hi in parts_of(k):
+                nc.sync.dma_start(
+                    weights[k][:, lo:hi],
+                    w[:, k * PIECE + lo : k * PIECE + hi].broadcast_to([SAMPLES, hi - lo]),
+                )
             if k == LAG:
                 nc.sync.dma_start(bias[:], b.broadcast_to([SAMPLES, PATCHES]))
 
@@ -80,8 +87,9 @@ def tile_patchy_layer_returnfullseq_kernel(tc, x, w, b, offs, out):
 
         def look_up(k):
             product[k] = ring.tile([SAMPLES, PIECE], F32, name="product")
-            picked = window[:].indirect(offsets[:, k * (PIECE // 16) : (k + 1) * (PIECE // 16)])
-            nc.vector.tensor_tensor(product[k][:], picked, weights[k][:], ALU.mult)
+            for lo, hi in parts_of(k):
+                picked = window[:].indirect(offsets[:, (k * PIECE + lo) // 16 : (k * PIECE + hi) // 16])
+                nc.vector.tensor_tensor(product[k][:, lo:hi], picked, weights[k][:, lo:hi], ALU.mult)
 
         run_sums = {}
 
@@ -122,11 +130,11 @@ def tile_patchy_layer_returnfullseq_kernel(tc, x, w, b, offs, out):
                 active[:].rearrange("c s r p -> c (s r p)"), v[:], SLOPE, v[:], ALU.mult, ALU.max
             )
             stretched = ring.tile([SAMPLES, PIECE_STEPS, STRETCH, PER_STEP], F32, name="stretched")
-            nc.scalar.activation(
-                stretched[:],
-                active[:].broadcast_to([SAMPLES, PIECE_STEPS, STRETCH, PER_STEP]),
-                FUNC.Copy,
-            )
+            repeated = active[:].broadcast_to([SAMPLES, PIECE_STEPS, STRETCH, PER_STEP])
+            if k == PIECES - 1:
+                nc.vector.tensor_copy(stretched[:], repeated)
+            else:
+                nc.scalar.activation(stretched[:], repeated, FUNC.Copy)
             nc.sync.dma_start(
                 out[:, k * PIECE_OUT : (k + 1) * PIECE_OUT],
                 stretched[:].rearrange("c s r p -> c (s r p)"),

@@ -16,139 +16,206 @@ PER_STEP = 8
 STRETCH = 8
 SLOPE = 0.3
 
-PIECE = 1024
-PIECES = ENTRIES // PIECE
-PIECE_PATCHES = PIECE // PLACES
-PIECE_STEPS = PIECE_PATCHES // PER_STEP
-PIECE_OUT = PIECE_PATCHES * STRETCH
+SIZES = (1024,) * 7 + (512, 512)
+ON_VECTOR = 2
+STARTS = tuple(sum(SIZES[:k]) for k in range(len(SIZES)))
+PIECES = len(SIZES)
+assert sum(SIZES) == ENTRIES
 
 RUNS = 128
-RUN = PIECE // RUNS
-PATCH_RUNS = PLACES // RUN
+BLOCK = 64
+BLOCKS = PATCHES // BLOCK
 
-HEAD = 256
-LAG = 3
+HEAD_BOUNDS = (0, 128, 384, SIZES[0])
 
 FLOPS = 2 * SAMPLES * ENTRIES
 
 
 def parts_of(k):
-    return ((0, HEAD), (HEAD, PIECE)) if k == 0 else ((0, PIECE),)
+    return tuple(zip(HEAD_BOUNDS[:-1], HEAD_BOUNDS[1:])) if k == 0 else ((0, SIZES[k]),)
 
 
 def tile_patchy_layer_returnfullseq_kernel(tc, x, w, b, offs, out):
     nc = tc.nc
     with (
         tc.tile_pool(name="held", bufs=1) as held,
-        tc.tile_pool(name="ring", bufs=LAG + 2) as ring,
         tc.psum_pool(name="psum", bufs=2) as psum,
-        tc.psum_pool(name="psum_waiting", bufs=LAG + 2) as psum_waiting,
     ):
         offsets = held.tile([SAMPLES, ENTRIES // 16], U16, name="offsets")
         nc.sync.dma_start(offsets[:], offs)
         window = held.tile([SAMPLES, POINTS], F32, name="window")
         nc.sync.dma_start(window[:], x)
-        weights = [held.tile([SAMPLES, PIECE], F32, name=f"weights{k}") for k in range(PIECES)]
+        weights = [held.tile([SAMPLES, SIZES[k]], F32, name=f"weights{k}") for k in range(PIECES)]
         bias = held.tile([SAMPLES, PATCHES], F32, name="bias")
         for k in range(PIECES):
             for lo, hi in parts_of(k):
                 nc.sync.dma_start(
                     weights[k][:, lo:hi],
-                    w[:, k * PIECE + lo : k * PIECE + hi].broadcast_to([SAMPLES, hi - lo]),
+                    w[:, STARTS[k] + lo : STARTS[k] + hi].broadcast_to([SAMPLES, hi - lo]),
                 )
-            if k == LAG:
+            if k == 0:
                 nc.sync.dma_start(bias[:], b.broadcast_to([SAMPLES, PATCHES]))
 
         identity = held.tile([SAMPLES, SAMPLES], F32, name="identity")
         make_identity(nc, identity[:])
-        run_of_patch = held.tile([RUNS, PIECE_PATCHES], F32, name="run_of_patch")
-        nc.gpsimd.memset(run_of_patch[:], 1.0)
-        nc.gpsimd.affine_select(
-            out=run_of_patch[:],
-            in_=run_of_patch[:],
-            pattern=[[-PATCH_RUNS, PIECE_PATCHES]],
-            compare_op=ALU.is_ge,
-            fill=0.0,
-            base=0,
-            channel_multiplier=1,
-        )
-        nc.gpsimd.affine_select(
-            out=run_of_patch[:],
-            in_=run_of_patch[:],
-            pattern=[[PATCH_RUNS, PIECE_PATCHES]],
-            compare_op=ALU.is_ge,
-            fill=0.0,
-            base=PATCH_RUNS - 1,
-            channel_multiplier=-1,
+
+        slope_sign = held.tile([2 * BLOCK, 1], F32, name="slope_sign")
+        nc.gpsimd.memset(slope_sign[:BLOCK], 1.0)
+        nc.gpsimd.memset(slope_sign[BLOCK:], -SLOPE)
+        unstack = held.tile([2 * BLOCK, BLOCK], F32, name="unstack")
+        nc.gpsimd.memset(unstack[:], 0.0)
+        for half, sign in ((0, 1.0), (1, -1.0)):
+            nc.gpsimd.affine_select(
+                out=unstack[:],
+                in_=unstack[:],
+                pattern=[[-1, BLOCK]],
+                compare_op=ALU.not_equal,
+                fill=sign,
+                base=-BLOCK * half,
+                channel_multiplier=1,
+            )
+
+        def make_run_of_patch(k):
+            patch_runs = PLACES * RUNS // SIZES[k]
+            place = STARTS[k] // PLACES % BLOCK
+            selector = held.tile([RUNS, 2, BLOCK], F32, name=f"run_of_patch{k}")
+            nc.gpsimd.memset(selector[:], 1.0)
+            nc.gpsimd.affine_select(
+                out=selector[:],
+                in_=selector[:],
+                pattern=[[0, 2], [-patch_runs, BLOCK]],
+                compare_op=ALU.is_ge,
+                fill=0.0,
+                base=patch_runs * place,
+                channel_multiplier=1,
+            )
+            nc.gpsimd.affine_select(
+                out=selector[:],
+                in_=selector[:],
+                pattern=[[0, 2], [patch_runs, BLOCK]],
+                compare_op=ALU.is_ge,
+                fill=0.0,
+                base=patch_runs - 1 - patch_runs * place,
+                channel_multiplier=-1,
+            )
+            return selector
+
+        run_of_patch = {}
+        for k in range(PIECES - ON_VECTOR):
+            key = (SIZES[k], STARTS[k] // PLACES % BLOCK)
+            if key not in run_of_patch:
+                run_of_patch[key] = make_run_of_patch(k)
+
+        bias_twice = held.tile([SAMPLES, BLOCKS, 2, BLOCK], F32, name="bias_twice")
+        nc.scalar.activation(
+            bias_twice[:],
+            bias[:].rearrange("c (n h q) -> c n h q", h=1, q=BLOCK).broadcast_to([SAMPLES, BLOCKS, 2, BLOCK]),
+            FUNC.Copy,
         )
 
         product = {}
-        sums = {}
 
         def look_up(k):
-            product[k] = ring.tile([SAMPLES, PIECE], F32, name="product")
+            product[k] = held.tile([SAMPLES, SIZES[k]], F32, name=f"product{k}")
             for lo, hi in parts_of(k):
-                picked = window[:].indirect(offsets[:, (k * PIECE + lo) // 16 : (k * PIECE + hi) // 16])
+                picked = window[:].indirect(offsets[:, (STARTS[k] + lo) // 16 : (STARTS[k] + hi) // 16])
                 nc.vector.tensor_tensor(product[k][:, lo:hi], picked, weights[k][:, lo:hi], ALU.mult)
 
+        def store(k, stretched):
+            nc.sync.dma_start(
+                out[:, STARTS[k] // PLACES * STRETCH : (STARTS[k] + SIZES[k]) // PLACES * STRETCH],
+                stretched[:].rearrange("c s r p -> c (s r p)"),
+            )
+
         run_sums = {}
+        terms = {}
 
         def sum_runs(k):
-            by_run = product[k][:].rearrange("c (m j) -> c m j", j=RUN)
+            run = SIZES[k] // RUNS
+            by_run = product[k][:].rearrange("c (m j) -> c m j", j=run)
             run_sums_psum = psum.tile([RUNS, SAMPLES], F32, name="run_sums_psum")
-            for j in range(RUN):
+            for j in range(run):
                 nc.tensor.matmul(
                     run_sums_psum[:],
                     lhsT=by_run[:, :, j],
                     rhs=identity[:],
                     start=(j == 0),
-                    stop=(j == RUN - 1),
+                    stop=(j == run - 1),
                     is_transpose=True,
                 )
-            run_sums[k] = ring.tile([RUNS, SAMPLES], F32, name="run_sums")
+            run_sums[k] = held.tile([RUNS, SAMPLES], F32, name=f"run_sums{k}")
             nc.scalar.activation(run_sums[k][:], run_sums_psum[:], FUNC.Copy)
 
-        def sum_patches(k):
-            sums[k] = psum_waiting.tile([SAMPLES, PIECE_PATCHES], F32, name="sums_psum")
+        def take_terms(k):
+            block, place = divmod(STARTS[k] // PLACES, BLOCK)
+            v_psum = psum.tile([2 * BLOCK, SAMPLES], F32, name="v_psum")
             nc.tensor.matmul(
-                sums[k][:], lhsT=run_sums[k][:], rhs=run_of_patch[:], start=True, stop=True
+                v_psum[:],
+                lhsT=bias_twice[:, block].rearrange("c h q -> c (h q)"),
+                rhs=identity[:],
+                start=True,
+                stop=False,
             )
+            nc.tensor.matmul(
+                v_psum[:],
+                lhsT=run_of_patch[(SIZES[k], place)][:].rearrange("m h q -> m (h q)"),
+                rhs=run_sums[k][:],
+                start=False,
+                stop=True,
+            )
+            terms[k] = held.tile([2 * BLOCK, SAMPLES], F32, name=f"terms{k}")
+            nc.scalar.activation(terms[k][:], v_psum[:], FUNC.Relu, scale=slope_sign[:, 0:1])
+
+        def stretch_and_store(k):
+            patches = SIZES[k] // PLACES
+            place = STARTS[k] // PLACES % BLOCK
+            active_psum = psum.tile([SAMPLES, BLOCK // PER_STEP, 1, PER_STEP], F32, name="active_psum")
+            active = active_psum[:, : patches // PER_STEP]
+            nc.tensor.matmul(
+                active.rearrange("c s r p -> c (s r p)"),
+                lhsT=terms[k][:],
+                rhs=unstack[:, place : place + patches],
+                start=True,
+                stop=True,
+            )
+            stretched = held.tile([SAMPLES, patches // PER_STEP, STRETCH, PER_STEP], F32, name=f"stretched{k}")
+            nc.scalar.activation(stretched[:], active.broadcast_to(stretched.shape), FUNC.Copy)
+            store(k, stretched)
+
+        sums = {}
+        v = {}
 
         def sum_on_vector(k):
-            sums[k] = ring.tile([SAMPLES, PIECE_PATCHES], F32, name="sums_sbuf")
+            sums[k] = held.tile([SAMPLES, SIZES[k] // PLACES], F32, name=f"sums{k}")
             nc.vector.tensor_reduce(
                 sums[k][:], product[k][:].rearrange("c (q i) -> c q i", i=PLACES), AXIS.X, ALU.add
             )
 
-        def finish(k):
-            v = ring.tile([SAMPLES, PIECE_PATCHES], F32, name="v")
+        def add_bias_on_vector(k):
+            patches = SIZES[k] // PLACES
+            first = STARTS[k] // PLACES
+            v[k] = held.tile([SAMPLES, patches // PER_STEP, 1, PER_STEP], F32, name=f"v{k}")
             nc.vector.tensor_tensor(
-                v[:], sums[k][:], bias[:, k * PIECE_PATCHES : (k + 1) * PIECE_PATCHES], ALU.add
-            )
-            active = ring.tile([SAMPLES, PIECE_STEPS, 1, PER_STEP], F32, name="active")
-            nc.vector.scalar_tensor_tensor(
-                active[:].rearrange("c s r p -> c (s r p)"), v[:], SLOPE, v[:], ALU.mult, ALU.max
-            )
-            stretched = ring.tile([SAMPLES, PIECE_STEPS, STRETCH, PER_STEP], F32, name="stretched")
-            repeated = active[:].broadcast_to([SAMPLES, PIECE_STEPS, STRETCH, PER_STEP])
-            if k == PIECES - 1:
-                nc.vector.tensor_copy(stretched[:], repeated)
-            else:
-                nc.scalar.activation(stretched[:], repeated, FUNC.Copy)
-            nc.sync.dma_start(
-                out[:, k * PIECE_OUT : (k + 1) * PIECE_OUT],
-                stretched[:].rearrange("c s r p -> c (s r p)"),
+                v[k][:].rearrange("c s r p -> c (s r p)"), sums[k][:], bias[:, first : first + patches], ALU.add
             )
 
-        last = PIECES - 1
-        for k in range(PIECES):
+        def stretch_and_store_on_vector(k):
+            steps = SIZES[k] // PLACES // PER_STEP
+            stretched = held.tile([SAMPLES, steps, STRETCH, PER_STEP], F32, name=f"stretched{k}")
+            for s in range(steps):
+                repeated = v[k][:, s].broadcast_to([SAMPLES, STRETCH, PER_STEP])
+                nc.vector.scalar_tensor_tensor(stretched[:, s], repeated, SLOPE, repeated, ALU.mult, ALU.max)
+            store(k, stretched)
+
+        beside = range(PIECES - ON_VECTOR)
+        for k in beside:
             look_up(k)
-            if k >= LAG:
-                finish(k - LAG)
-            if k < last:
-                sum_runs(k)
+            sum_runs(k)
             if k >= 1:
-                sum_patches(k - 1)
-        sum_on_vector(last)
-        for k in range(PIECES - LAG, PIECES):
-            finish(k)
+                stretch_and_store(k - 1)
+            take_terms(k)
+        stretch_and_store(beside[-1])
+        on_vector = range(PIECES - ON_VECTOR, PIECES)
+        for step in (look_up, sum_on_vector, add_bias_on_vector, stretch_and_store_on_vector):
+            for k in on_vector:
+                step(k)

@@ -16,23 +16,24 @@ PER_STEP = 8
 STRETCH = 8
 SLOPE = 0.3
 
-SIZES = (1024,) * 7 + (512, 512)
-ON_VECTOR = 2
+SIZES = (1024,) * 8
 STARTS = tuple(sum(SIZES[:k]) for k in range(len(SIZES)))
 PIECES = len(SIZES)
 assert sum(SIZES) == ENTRIES
 
 RUNS = 128
-BLOCK = 64
-BLOCKS = PATCHES // BLOCK
+GROUP = 32
+GROUPS = 128 // GROUP
 
 HEAD_BOUNDS = (0, 128, 384, SIZES[0])
+TAIL_BOUNDS = (0, SIZES[-1] // 2, SIZES[-1])
 
 FLOPS = 2 * SAMPLES * ENTRIES
 
 
 def parts_of(k):
-    return tuple(zip(HEAD_BOUNDS[:-1], HEAD_BOUNDS[1:])) if k == 0 else ((0, SIZES[k]),)
+    bounds = HEAD_BOUNDS if k == 0 else TAIL_BOUNDS if k == PIECES - 1 else (0, SIZES[k])
+    return tuple(zip(bounds[:-1], bounds[1:]))
 
 
 def tile_patchy_layer_returnfullseq_kernel(tc, x, w, b, offs, out):
@@ -59,61 +60,58 @@ def tile_patchy_layer_returnfullseq_kernel(tc, x, w, b, offs, out):
         identity = held.tile([SAMPLES, SAMPLES], F32, name="identity")
         make_identity(nc, identity[:])
 
-        slope_sign = held.tile([2 * BLOCK, 1], F32, name="slope_sign")
-        nc.gpsimd.memset(slope_sign[:BLOCK], 1.0)
-        nc.gpsimd.memset(slope_sign[BLOCK:], -SLOPE)
-        unstack = held.tile([2 * BLOCK, BLOCK], F32, name="unstack")
-        nc.gpsimd.memset(unstack[:], 0.0)
-        for half, sign in ((0, 1.0), (1, -1.0)):
+        slope_sign = held.tile([128, 1], F32, name="slope_sign")
+        nc.vector.memset(slope_sign[:], 1.0)
+        nc.vector.memset(slope_sign[GROUP : 2 * GROUP], -SLOPE)
+        unstack = held.tile([128, GROUP], F32, name="unstack")
+        nc.vector.memset(unstack[:], 0.0)
+        for group, sign in ((0, 1.0), (1, -1.0)):
             nc.gpsimd.affine_select(
                 out=unstack[:],
                 in_=unstack[:],
-                pattern=[[-1, BLOCK]],
+                pattern=[[-1, GROUP]],
                 compare_op=ALU.not_equal,
                 fill=sign,
-                base=-BLOCK * half,
+                base=-GROUP * group,
                 channel_multiplier=1,
             )
-
-        def make_run_of_patch(k):
-            patch_runs = PLACES * RUNS // SIZES[k]
-            place = STARTS[k] // PLACES % BLOCK
-            selector = held.tile([RUNS, 2, BLOCK], F32, name=f"run_of_patch{k}")
-            nc.gpsimd.memset(selector[:], 1.0)
+        run_of_patch = {}
+        for size in sorted(set(SIZES[:-1])):
+            patch_runs = PLACES * RUNS // size
+            selector = held.tile([RUNS, GROUPS, GROUP], F32, name=f"run_of_patch{size}")
+            nc.vector.memset(selector[:], 1.0)
             nc.gpsimd.affine_select(
                 out=selector[:],
                 in_=selector[:],
-                pattern=[[0, 2], [-patch_runs, BLOCK]],
+                pattern=[[0, GROUPS], [-patch_runs, GROUP]],
                 compare_op=ALU.is_ge,
                 fill=0.0,
-                base=patch_runs * place,
+                base=0,
                 channel_multiplier=1,
             )
             nc.gpsimd.affine_select(
                 out=selector[:],
                 in_=selector[:],
-                pattern=[[0, 2], [patch_runs, BLOCK]],
+                pattern=[[0, GROUPS], [patch_runs, GROUP]],
                 compare_op=ALU.is_ge,
                 fill=0.0,
-                base=patch_runs - 1 - patch_runs * place,
+                base=patch_runs - 1,
                 channel_multiplier=-1,
             )
-            return selector
+            run_of_patch[size] = selector
 
-        run_of_patch = {}
-        for k in range(PIECES - ON_VECTOR):
-            key = (SIZES[k], STARTS[k] // PLACES % BLOCK)
-            if key not in run_of_patch:
-                run_of_patch[key] = make_run_of_patch(k)
-
-        bias_twice = held.tile([SAMPLES, BLOCKS, 2, BLOCK], F32, name="bias_twice")
-        nc.scalar.activation(
-            bias_twice[:],
-            bias[:].rearrange("c (n h q) -> c n h q", h=1, q=BLOCK).broadcast_to([SAMPLES, BLOCKS, 2, BLOCK]),
-            FUNC.Copy,
-        )
+        bias_groups = held.tile([SAMPLES, PIECES - 1, GROUPS, GROUP], F32, name="bias_groups")
+        for k in range(PIECES - 1):
+            first = STARTS[k] // PLACES
+            nc.scalar.activation(
+                bias_groups[:, k],
+                bias[:, first : first + GROUP].unsqueeze(1).broadcast_to([SAMPLES, GROUPS, GROUP]),
+                FUNC.Copy,
+            )
 
         product = {}
+        run_sums = {}
+        terms = {}
 
         def look_up(k):
             product[k] = held.tile([SAMPLES, SIZES[k]], F32, name=f"product{k}")
@@ -121,14 +119,11 @@ def tile_patchy_layer_returnfullseq_kernel(tc, x, w, b, offs, out):
                 picked = window[:].indirect(offsets[:, (STARTS[k] + lo) // 16 : (STARTS[k] + hi) // 16])
                 nc.vector.tensor_tensor(product[k][:, lo:hi], picked, weights[k][:, lo:hi], ALU.mult)
 
-        def store(k, stretched):
+        def store(first, stretched):
+            columns = stretched.shape[1] * STRETCH * PER_STEP
             nc.sync.dma_start(
-                out[:, STARTS[k] // PLACES * STRETCH : (STARTS[k] + SIZES[k]) // PLACES * STRETCH],
-                stretched[:].rearrange("c s r p -> c (s r p)"),
+                out[:, first * STRETCH : first * STRETCH + columns], stretched.rearrange("c s r p -> c (s r p)")
             )
-
-        run_sums = {}
-        terms = {}
 
         def sum_runs(k):
             run = SIZES[k] // RUNS
@@ -147,75 +142,68 @@ def tile_patchy_layer_returnfullseq_kernel(tc, x, w, b, offs, out):
             nc.scalar.activation(run_sums[k][:], run_sums_psum[:], FUNC.Copy)
 
         def take_terms(k):
-            block, place = divmod(STARTS[k] // PLACES, BLOCK)
-            v_psum = psum.tile([2 * BLOCK, SAMPLES], F32, name="v_psum")
+            v_psum = psum.tile([128, SAMPLES], F32, name="v_psum")
             nc.tensor.matmul(
                 v_psum[:],
-                lhsT=bias_twice[:, block].rearrange("c h q -> c (h q)"),
+                lhsT=bias_groups[:, k].rearrange("c g q -> c (g q)"),
                 rhs=identity[:],
                 start=True,
                 stop=False,
             )
             nc.tensor.matmul(
                 v_psum[:],
-                lhsT=run_of_patch[(SIZES[k], place)][:].rearrange("m h q -> m (h q)"),
+                lhsT=run_of_patch[SIZES[k]][:].rearrange("m g q -> m (g q)"),
                 rhs=run_sums[k][:],
                 start=False,
                 stop=True,
             )
-            terms[k] = held.tile([2 * BLOCK, SAMPLES], F32, name=f"terms{k}")
+            terms[k] = held.tile([128, SAMPLES], F32, name=f"terms{k}")
             nc.scalar.activation(terms[k][:], v_psum[:], FUNC.Relu, scale=slope_sign[:, 0:1])
 
         def stretch_and_store(k):
             patches = SIZES[k] // PLACES
-            place = STARTS[k] // PLACES % BLOCK
-            active_psum = psum.tile([SAMPLES, BLOCK // PER_STEP, 1, PER_STEP], F32, name="active_psum")
+            active_psum = psum.tile([SAMPLES, GROUP // PER_STEP, 1, PER_STEP], F32, name="active_psum")
             active = active_psum[:, : patches // PER_STEP]
             nc.tensor.matmul(
                 active.rearrange("c s r p -> c (s r p)"),
                 lhsT=terms[k][:],
-                rhs=unstack[:, place : place + patches],
+                rhs=unstack[:, :patches],
                 start=True,
                 stop=True,
             )
             stretched = held.tile([SAMPLES, patches // PER_STEP, STRETCH, PER_STEP], F32, name=f"stretched{k}")
             nc.scalar.activation(stretched[:], active.broadcast_to(stretched.shape), FUNC.Copy)
-            store(k, stretched)
+            store(STARTS[k] // PLACES, stretched[:])
 
-        sums = {}
-        v = {}
-
-        def sum_on_vector(k):
-            sums[k] = held.tile([SAMPLES, SIZES[k] // PLACES], F32, name=f"sums{k}")
-            nc.vector.tensor_reduce(
-                sums[k][:], product[k][:].rearrange("c (q i) -> c q i", i=PLACES), AXIS.X, ALU.add
-            )
-
-        def add_bias_on_vector(k):
+        def finish_on_vector(k):
             patches = SIZES[k] // PLACES
             first = STARTS[k] // PLACES
-            v[k] = held.tile([SAMPLES, patches // PER_STEP, 1, PER_STEP], F32, name=f"v{k}")
-            nc.vector.tensor_tensor(
-                v[k][:].rearrange("c s r p -> c (s r p)"), sums[k][:], bias[:, first : first + patches], ALU.add
-            )
+            halves = tuple((lo // PLACES, hi // PLACES) for lo, hi in parts_of(k))
+            sums = held.tile([SAMPLES, patches], F32, name="sums")
+            by_patch = product[k][:].rearrange("c (q i) -> c q i", i=PLACES)
+            for lo, hi in halves:
+                nc.vector.tensor_reduce(sums[:, lo:hi], by_patch[:, lo:hi], AXIS.X, ALU.add)
+            v = held.tile([SAMPLES, patches], F32, name="v")
+            for lo, hi in halves:
+                nc.vector.tensor_tensor(v[:, lo:hi], sums[:, lo:hi], bias[:, first + lo : first + hi], ALU.add)
+            stretched = held.tile([SAMPLES, patches // PER_STEP, STRETCH, PER_STEP], F32, name=f"stretched{k}")
+            for lo, hi in halves:
+                for s in range(lo // PER_STEP, hi // PER_STEP):
+                    repeated = (
+                        v[:, s * PER_STEP : (s + 1) * PER_STEP]
+                        .unsqueeze(1)
+                        .broadcast_to([SAMPLES, STRETCH, PER_STEP])
+                    )
+                    nc.vector.scalar_tensor_tensor(stretched[:, s], repeated, SLOPE, repeated, ALU.mult, ALU.max)
+                store(first + lo, stretched[:, lo // PER_STEP : hi // PER_STEP])
 
-        def stretch_and_store_on_vector(k):
-            steps = SIZES[k] // PLACES // PER_STEP
-            stretched = held.tile([SAMPLES, steps, STRETCH, PER_STEP], F32, name=f"stretched{k}")
-            for s in range(steps):
-                repeated = v[k][:, s].broadcast_to([SAMPLES, STRETCH, PER_STEP])
-                nc.vector.scalar_tensor_tensor(stretched[:, s], repeated, SLOPE, repeated, ALU.mult, ALU.max)
-            store(k, stretched)
-
-        beside = range(PIECES - ON_VECTOR)
-        for k in beside:
+        last = PIECES - 1
+        for k in range(last):
             look_up(k)
             sum_runs(k)
             if k >= 1:
                 stretch_and_store(k - 1)
             take_terms(k)
-        stretch_and_store(beside[-1])
-        on_vector = range(PIECES - ON_VECTOR, PIECES)
-        for step in (look_up, sum_on_vector, add_bias_on_vector, stretch_and_store_on_vector):
-            for k in on_vector:
-                step(k)
+        stretch_and_store(last - 1)
+        look_up(last)
+        finish_on_vector(last)

@@ -16,24 +16,19 @@ PER_STEP = 8
 STRETCH = 8
 SLOPE = 0.3
 
-SIZES = (1024,) * 8
-STARTS = tuple(sum(SIZES[:k]) for k in range(len(SIZES)))
-PIECES = len(SIZES)
-assert sum(SIZES) == ENTRIES
+LOOKUP_BOUNDS = (0, 2048, 4096, 6144, 7168, 8192)
+LOOKUPS = tuple(zip(LOOKUP_BOUNDS[:-1], LOOKUP_BOUNDS[1:]))
+
+PIECE = 1024
+PIECES = ENTRIES // PIECE
 
 RUNS = 128
-GROUP = 32
+RUN = PIECE // RUNS
+PATCH_RUNS = PLACES // RUN
+GROUP = PIECE // PLACES
 GROUPS = 128 // GROUP
 
-HEAD_BOUNDS = (0, 128, 384, SIZES[0])
-TAIL_BOUNDS = (0, SIZES[-1] // 2, SIZES[-1])
-
 FLOPS = 2 * SAMPLES * ENTRIES
-
-
-def parts_of(k):
-    bounds = HEAD_BOUNDS if k == 0 else TAIL_BOUNDS if k == PIECES - 1 else (0, SIZES[k])
-    return tuple(zip(bounds[:-1], bounds[1:]))
 
 
 def tile_patchy_layer_returnfullseq_kernel(tc, x, w, b, offs, out):
@@ -46,15 +41,11 @@ def tile_patchy_layer_returnfullseq_kernel(tc, x, w, b, offs, out):
         nc.sync.dma_start(offsets[:], offs)
         window = held.tile([SAMPLES, POINTS], F32, name="window")
         nc.sync.dma_start(window[:], x)
-        weights = [held.tile([SAMPLES, SIZES[k]], F32, name=f"weights{k}") for k in range(PIECES)]
+        weights = held.tile([SAMPLES, ENTRIES], F32, name="weights")
         bias = held.tile([SAMPLES, PATCHES], F32, name="bias")
-        for k in range(PIECES):
-            for lo, hi in parts_of(k):
-                nc.sync.dma_start(
-                    weights[k][:, lo:hi],
-                    w[:, STARTS[k] + lo : STARTS[k] + hi].broadcast_to([SAMPLES, hi - lo]),
-                )
-            if k == 0:
+        for lo, hi in LOOKUPS:
+            nc.sync.dma_start(weights[:, lo:hi], w[:, lo:hi].broadcast_to([SAMPLES, hi - lo]))
+            if lo == 0:
                 nc.sync.dma_start(bias[:], b.broadcast_to([SAMPLES, PATCHES]))
 
         identity = held.tile([SAMPLES, SAMPLES], F32, name="identity")
@@ -75,49 +66,41 @@ def tile_patchy_layer_returnfullseq_kernel(tc, x, w, b, offs, out):
                 base=-GROUP * group,
                 channel_multiplier=1,
             )
-        run_of_patch = {}
-        for size in sorted(set(SIZES[:-1])):
-            patch_runs = PLACES * RUNS // size
-            selector = held.tile([RUNS, GROUPS, GROUP], F32, name=f"run_of_patch{size}")
-            nc.vector.memset(selector[:], 1.0)
-            nc.gpsimd.affine_select(
-                out=selector[:],
-                in_=selector[:],
-                pattern=[[0, GROUPS], [-patch_runs, GROUP]],
-                compare_op=ALU.is_ge,
-                fill=0.0,
-                base=0,
-                channel_multiplier=1,
-            )
-            nc.gpsimd.affine_select(
-                out=selector[:],
-                in_=selector[:],
-                pattern=[[0, GROUPS], [patch_runs, GROUP]],
-                compare_op=ALU.is_ge,
-                fill=0.0,
-                base=patch_runs - 1,
-                channel_multiplier=-1,
-            )
-            run_of_patch[size] = selector
+        run_of_patch = held.tile([RUNS, GROUPS, GROUP], F32, name="run_of_patch")
+        nc.vector.memset(run_of_patch[:], 1.0)
+        nc.gpsimd.affine_select(
+            out=run_of_patch[:],
+            in_=run_of_patch[:],
+            pattern=[[0, GROUPS], [-PATCH_RUNS, GROUP]],
+            compare_op=ALU.is_ge,
+            fill=0.0,
+            base=0,
+            channel_multiplier=1,
+        )
+        nc.gpsimd.affine_select(
+            out=run_of_patch[:],
+            in_=run_of_patch[:],
+            pattern=[[0, GROUPS], [PATCH_RUNS, GROUP]],
+            compare_op=ALU.is_ge,
+            fill=0.0,
+            base=PATCH_RUNS - 1,
+            channel_multiplier=-1,
+        )
 
-        bias_groups = held.tile([SAMPLES, PIECES - 1, GROUPS, GROUP], F32, name="bias_groups")
-        for k in range(PIECES - 1):
-            first = STARTS[k] // PLACES
-            nc.scalar.activation(
-                bias_groups[:, k],
-                bias[:, first : first + GROUP].unsqueeze(1).broadcast_to([SAMPLES, GROUPS, GROUP]),
-                FUNC.Copy,
-            )
+        bias_groups = held.tile([SAMPLES, PIECES, GROUPS, GROUP], F32, name="bias_groups")
+        nc.scalar.activation(
+            bias_groups[:],
+            bias[:].rearrange("c (k g q) -> c k g q", g=1, q=GROUP).broadcast_to(bias_groups.shape),
+            FUNC.Copy,
+        )
 
-        product = {}
+        product = held.tile([SAMPLES, ENTRIES], F32, name="product")
         run_sums = {}
         terms = {}
 
-        def look_up(k):
-            product[k] = held.tile([SAMPLES, SIZES[k]], F32, name=f"product{k}")
-            for lo, hi in parts_of(k):
-                picked = window[:].indirect(offsets[:, (STARTS[k] + lo) // 16 : (STARTS[k] + hi) // 16])
-                nc.vector.tensor_tensor(product[k][:, lo:hi], picked, weights[k][:, lo:hi], ALU.mult)
+        def look_up(lo, hi):
+            picked = window[:].indirect(offsets[:, lo // 16 : hi // 16])
+            nc.vector.tensor_tensor(product[:, lo:hi], picked, weights[:, lo:hi], ALU.mult)
 
         def store(first, stretched):
             columns = stretched.shape[1] * STRETCH * PER_STEP
@@ -126,16 +109,15 @@ def tile_patchy_layer_returnfullseq_kernel(tc, x, w, b, offs, out):
             )
 
         def sum_runs(k):
-            run = SIZES[k] // RUNS
-            by_run = product[k][:].rearrange("c (m j) -> c m j", j=run)
+            by_run = product[:, k * PIECE : (k + 1) * PIECE].rearrange("c (m j) -> c m j", j=RUN)
             run_sums_psum = psum.tile([RUNS, SAMPLES], F32, name="run_sums_psum")
-            for j in range(run):
+            for j in range(RUN):
                 nc.tensor.matmul(
                     run_sums_psum[:],
                     lhsT=by_run[:, :, j],
                     rhs=identity[:],
                     start=(j == 0),
-                    stop=(j == run - 1),
+                    stop=(j == RUN - 1),
                     is_transpose=True,
                 )
             run_sums[k] = held.tile([RUNS, SAMPLES], F32, name=f"run_sums{k}")
@@ -152,7 +134,7 @@ def tile_patchy_layer_returnfullseq_kernel(tc, x, w, b, offs, out):
             )
             nc.tensor.matmul(
                 v_psum[:],
-                lhsT=run_of_patch[SIZES[k]][:].rearrange("m g q -> m (g q)"),
+                lhsT=run_of_patch[:].rearrange("m g q -> m (g q)"),
                 rhs=run_sums[k][:],
                 start=False,
                 stop=True,
@@ -161,26 +143,20 @@ def tile_patchy_layer_returnfullseq_kernel(tc, x, w, b, offs, out):
             nc.scalar.activation(terms[k][:], v_psum[:], FUNC.Relu, scale=slope_sign[:, 0:1])
 
         def stretch_and_store(k):
-            patches = SIZES[k] // PLACES
-            active_psum = psum.tile([SAMPLES, GROUP // PER_STEP, 1, PER_STEP], F32, name="active_psum")
-            active = active_psum[:, : patches // PER_STEP]
+            active = psum.tile([SAMPLES, GROUP // PER_STEP, 1, PER_STEP], F32, name="active")
             nc.tensor.matmul(
-                active.rearrange("c s r p -> c (s r p)"),
-                lhsT=terms[k][:],
-                rhs=unstack[:, :patches],
-                start=True,
-                stop=True,
+                active[:].rearrange("c s r p -> c (s r p)"), lhsT=terms[k][:], rhs=unstack[:], start=True, stop=True
             )
-            stretched = held.tile([SAMPLES, patches // PER_STEP, STRETCH, PER_STEP], F32, name=f"stretched{k}")
-            nc.scalar.activation(stretched[:], active.broadcast_to(stretched.shape), FUNC.Copy)
-            store(STARTS[k] // PLACES, stretched[:])
+            stretched = held.tile([SAMPLES, GROUP // PER_STEP, STRETCH, PER_STEP], F32, name=f"stretched{k}")
+            nc.scalar.activation(stretched[:], active[:].broadcast_to(stretched.shape), FUNC.Copy)
+            store(k * GROUP, stretched[:])
 
         def finish_on_vector(k):
-            patches = SIZES[k] // PLACES
-            first = STARTS[k] // PLACES
-            halves = tuple((lo // PLACES, hi // PLACES) for lo, hi in parts_of(k))
+            patches = GROUP
+            first = k * GROUP
+            halves = ((0, patches // 2), (patches // 2, patches))
             sums = held.tile([SAMPLES, patches], F32, name="sums")
-            by_patch = product[k][:].rearrange("c (q i) -> c q i", i=PLACES)
+            by_patch = product[:, k * PIECE : (k + 1) * PIECE].rearrange("c (q i) -> c q i", i=PLACES)
             for lo, hi in halves:
                 nc.vector.tensor_reduce(sums[:, lo:hi], by_patch[:, lo:hi], AXIS.X, ALU.add)
             v = held.tile([SAMPLES, patches], F32, name="v")
@@ -198,12 +174,13 @@ def tile_patchy_layer_returnfullseq_kernel(tc, x, w, b, offs, out):
                 store(first + lo, stretched[:, lo // PER_STEP : hi // PER_STEP])
 
         last = PIECES - 1
-        for k in range(last):
-            look_up(k)
-            sum_runs(k)
-            if k >= 1:
-                stretch_and_store(k - 1)
-            take_terms(k)
+        for lo, hi in LOOKUPS:
+            look_up(lo, hi)
+            for k in range(last):
+                if lo < (k + 1) * PIECE <= hi:
+                    sum_runs(k)
+                    if k >= 1:
+                        stretch_and_store(k - 1)
+                    take_terms(k)
         stretch_and_store(last - 1)
-        look_up(last)
         finish_on_vector(last)

@@ -151,6 +151,19 @@ def tile_patchy_layer_returnfullseq_kernel(tc, x, w, b, offs, out):
             nc.scalar.activation(stretched[:], active[:].broadcast_to(stretched.shape), FUNC.Copy)
             store(k * GROUP, stretched[:])
 
+        def finish_the_short_way(k):
+            sums = psum.tile([SAMPLES, GROUP], F32, name="sums")
+            nc.tensor.matmul(sums[:], lhsT=run_sums[k][:], rhs=run_of_patch[:, 0], start=True, stop=True)
+            v = held.tile([SAMPLES, GROUP], F32, name="v_short")
+            nc.vector.tensor_tensor(v[:], sums[:], bias[:, k * GROUP : (k + 1) * GROUP], ALU.add)
+            active = held.tile([SAMPLES, GROUP // PER_STEP, 1, PER_STEP], F32, name="active_short")
+            nc.vector.scalar_tensor_tensor(
+                active[:].rearrange("c s r p -> c (s r p)"), v[:], SLOPE, v[:], ALU.mult, ALU.max
+            )
+            stretched = held.tile([SAMPLES, GROUP // PER_STEP, STRETCH, PER_STEP], F32, name=f"stretched{k}")
+            nc.scalar.activation(stretched[:], active[:].broadcast_to(stretched.shape), FUNC.Copy)
+            store(k * GROUP, stretched[:])
+
         def finish_on_vector(k):
             patches = GROUP
             first = k * GROUP
@@ -181,6 +194,7 @@ def tile_patchy_layer_returnfullseq_kernel(tc, x, w, b, offs, out):
                     sum_runs(k)
                     if k >= 1:
                         stretch_and_store(k - 1)
-                    take_terms(k)
-        stretch_and_store(last - 1)
+                    if k < last - 1:
+                        take_terms(k)
+        finish_the_short_way(last - 1)
         finish_on_vector(last)

@@ -16,11 +16,15 @@ PER_STEP = 8
 STRETCH = 8
 SLOPE = 0.3
 
-LOOKUP_BOUNDS = (0, 2048, 4096, 6144, 7168, 8192)
+LOOKUP_BOUNDS = (0, 1024, 2048, 3072, 4096, 5120, 6144, 7168, 7680, 8192)
 LOOKUPS = tuple(zip(LOOKUP_BOUNDS[:-1], LOOKUP_BOUNDS[1:]))
 
 PIECE = 1024
 PIECES = ENTRIES // PIECE
+HALF = PIECE // 2
+LONG_WAY = 6
+
+LOAD = 2048
 
 RUNS = 128
 RUN = PIECE // RUNS
@@ -43,7 +47,8 @@ def tile_patchy_layer_returnfullseq_kernel(tc, x, w, b, offs, out):
         nc.sync.dma_start(window[:], x)
         weights = held.tile([SAMPLES, ENTRIES], F32, name="weights")
         bias = held.tile([SAMPLES, PATCHES], F32, name="bias")
-        for lo, hi in LOOKUPS:
+        for lo in range(0, ENTRIES, LOAD):
+            hi = lo + LOAD
             nc.sync.dma_start(weights[:, lo:hi], w[:, lo:hi].broadcast_to([SAMPLES, hi - lo]))
             if lo == 0:
                 nc.sync.dma_start(bias[:], b.broadcast_to([SAMPLES, PATCHES]))
@@ -87,6 +92,10 @@ def tile_patchy_layer_returnfullseq_kernel(tc, x, w, b, offs, out):
             channel_multiplier=-1,
         )
 
+        run_of_half_patch = held.tile([RUNS, GROUP // 2], F32, name="run_of_half_patch")
+        by_pair = run_of_patch[:, 0].rearrange("m (q h) -> m q h", h=2)
+        nc.vector.tensor_tensor(run_of_half_patch[:], by_pair[:, :, 0], by_pair[:, :, 1], ALU.add)
+
         bias_groups = held.tile([SAMPLES, PIECES, GROUPS, GROUP], F32, name="bias_groups")
         nc.scalar.activation(
             bias_groups[:],
@@ -108,16 +117,17 @@ def tile_patchy_layer_returnfullseq_kernel(tc, x, w, b, offs, out):
                 out[:, first * STRETCH : first * STRETCH + columns], stretched.rearrange("c s r p -> c (s r p)")
             )
 
-        def sum_runs(k):
-            by_run = product[:, k * PIECE : (k + 1) * PIECE].rearrange("c (m j) -> c m j", j=RUN)
+        def sum_runs(k, lo, hi):
+            run = (hi - lo) // RUNS
+            by_run = product[:, lo:hi].rearrange("c (m j) -> c m j", j=run)
             run_sums_psum = psum.tile([RUNS, SAMPLES], F32, name="run_sums_psum")
-            for j in range(RUN):
+            for j in range(run):
                 nc.tensor.matmul(
                     run_sums_psum[:],
                     lhsT=by_run[:, :, j],
                     rhs=identity[:],
                     start=(j == 0),
-                    stop=(j == RUN - 1),
+                    stop=(j == run - 1),
                     is_transpose=True,
                 )
             run_sums[k] = held.tile([RUNS, SAMPLES], F32, name=f"run_sums{k}")
@@ -151,50 +161,46 @@ def tile_patchy_layer_returnfullseq_kernel(tc, x, w, b, offs, out):
             nc.scalar.activation(stretched[:], active[:].broadcast_to(stretched.shape), FUNC.Copy)
             store(k * GROUP, stretched[:])
 
-        def finish_the_short_way(k):
-            sums = psum.tile([SAMPLES, GROUP], F32, name="sums")
-            nc.tensor.matmul(sums[:], lhsT=run_sums[k][:], rhs=run_of_patch[:, 0], start=True, stop=True)
-            v = held.tile([SAMPLES, GROUP], F32, name="v_short")
-            nc.vector.tensor_tensor(v[:], sums[:], bias[:, k * GROUP : (k + 1) * GROUP], ALU.add)
-            active = held.tile([SAMPLES, GROUP // PER_STEP, 1, PER_STEP], F32, name="active_short")
-            nc.vector.scalar_tensor_tensor(
-                active[:].rearrange("c s r p -> c (s r p)"), v[:], SLOPE, v[:], ALU.mult, ALU.max
-            )
-            stretched = held.tile([SAMPLES, GROUP // PER_STEP, STRETCH, PER_STEP], F32, name=f"stretched{k}")
-            nc.scalar.activation(stretched[:], active[:].broadcast_to(stretched.shape), FUNC.Copy)
-            store(k * GROUP, stretched[:])
-
-        def finish_on_vector(k):
-            patches = GROUP
-            first = k * GROUP
-            halves = ((0, patches // 2), (patches // 2, patches))
-            sums = held.tile([SAMPLES, patches], F32, name="sums")
-            by_patch = product[:, k * PIECE : (k + 1) * PIECE].rearrange("c (q i) -> c q i", i=PLACES)
-            for lo, hi in halves:
-                nc.vector.tensor_reduce(sums[:, lo:hi], by_patch[:, lo:hi], AXIS.X, ALU.add)
-            v = held.tile([SAMPLES, patches], F32, name="v")
-            for lo, hi in halves:
-                nc.vector.tensor_tensor(v[:, lo:hi], sums[:, lo:hi], bias[:, first + lo : first + hi], ALU.add)
-            stretched = held.tile([SAMPLES, patches // PER_STEP, STRETCH, PER_STEP], F32, name=f"stretched{k}")
-            for lo, hi in halves:
-                for s in range(lo // PER_STEP, hi // PER_STEP):
-                    repeated = (
-                        v[:, s * PER_STEP : (s + 1) * PER_STEP]
-                        .unsqueeze(1)
-                        .broadcast_to([SAMPLES, STRETCH, PER_STEP])
-                    )
-                    nc.vector.scalar_tensor_tensor(stretched[:, s], repeated, SLOPE, repeated, ALU.mult, ALU.max)
-                store(first + lo, stretched[:, lo // PER_STEP : hi // PER_STEP])
-
-        last = PIECES - 1
         for lo, hi in LOOKUPS:
             look_up(lo, hi)
-            for k in range(last):
+            for k in range(LONG_WAY):
                 if lo < (k + 1) * PIECE <= hi:
-                    sum_runs(k)
+                    sum_runs(k, k * PIECE, (k + 1) * PIECE)
                     if k >= 1:
                         stretch_and_store(k - 1)
-                    if k < last - 1:
-                        take_terms(k)
-        finish_the_short_way(last - 1)
-        finish_on_vector(last)
+                    take_terms(k)
+        stretch_and_store(LONG_WAY - 1)
+
+        late = LONG_WAY * PIECE // PLACES
+        own = PATCHES - GROUP // 2
+        sums_late = psum.tile([SAMPLES, own - late], F32, name="sums_late")
+        half = ENTRIES - HALF
+        for name, lo, hi, selector in (
+            ("late_piece", LONG_WAY * PIECE, (LONG_WAY + 1) * PIECE, run_of_patch[:, 0]),
+            ("late_half", (LONG_WAY + 1) * PIECE, half, run_of_half_patch[:]),
+        ):
+            sum_runs(name, lo, hi)
+            columns = slice(lo // PLACES - late, hi // PLACES - late)
+            nc.tensor.matmul(sums_late[:, columns], lhsT=run_sums[name][:], rhs=selector, start=True, stop=True)
+
+        sums_own = held.tile([SAMPLES, PATCHES - own], F32, name="sums_own")
+        by_patch = product[:, half:].rearrange("c (q i) -> c q i", i=PLACES)
+        nc.vector.tensor_reduce(sums_own[:], by_patch, AXIS.X, ALU.add)
+        v_late = held.tile([SAMPLES, own - late], F32, name="v_late")
+        nc.vector.tensor_tensor(v_late[:], sums_late[:], bias[:, late:own], ALU.add)
+        v_own = held.tile([SAMPLES, PATCHES - own], F32, name="v_own")
+        nc.vector.tensor_tensor(v_own[:], sums_own[:], bias[:, own:], ALU.add)
+        active_late = held.tile([SAMPLES, (own - late) // PER_STEP, 1, PER_STEP], F32, name="active_late")
+        nc.vector.scalar_tensor_tensor(
+            active_late[:].rearrange("c s r p -> c (s r p)"), v_late[:], SLOPE, v_late[:], ALU.mult, ALU.max
+        )
+        stretched_late = held.tile([SAMPLES, (own - late) // PER_STEP, STRETCH, PER_STEP], F32, name="stretched_late")
+        nc.scalar.activation(stretched_late[:], active_late[:].broadcast_to(stretched_late.shape), FUNC.Copy)
+        store(late, stretched_late[:])
+        stretched_own = held.tile([SAMPLES, (PATCHES - own) // PER_STEP, STRETCH, PER_STEP], F32, name="stretched_own")
+        for s in range((PATCHES - own) // PER_STEP):
+            repeated = (
+                v_own[:, s * PER_STEP : (s + 1) * PER_STEP].unsqueeze(1).broadcast_to([SAMPLES, STRETCH, PER_STEP])
+            )
+            nc.vector.scalar_tensor_tensor(stretched_own[:, s], repeated, SLOPE, repeated, ALU.mult, ALU.max)
+        store(own, stretched_own[:])

@@ -16,7 +16,7 @@ PER_STEP = 8
 STRETCH = 8
 SLOPE = 0.3
 
-LOOKUP_BOUNDS = (0, 1024, 2048, 3072, 4096, 5120, 6144, 7168, 7680, 8192)
+LOOKUP_BOUNDS = (0, 1024, 2048, 3072, 4096, 5120, 6144, 7168, 7680, 7936, 8192)
 LOOKUPS = tuple(zip(LOOKUP_BOUNDS[:-1], LOOKUP_BOUNDS[1:]))
 
 PIECE = 1024
@@ -171,36 +171,46 @@ def tile_patchy_layer_returnfullseq_kernel(tc, x, w, b, offs, out):
                     take_terms(k)
         stretch_and_store(LONG_WAY - 1)
 
-        late = LONG_WAY * PIECE // PLACES
-        own = PATCHES - GROUP // 2
-        sums_late = psum.tile([SAMPLES, own - late], F32, name="sums_late")
-        half = ENTRIES - HALF
-        for name, lo, hi, selector in (
-            ("late_piece", LONG_WAY * PIECE, (LONG_WAY + 1) * PIECE, run_of_patch[:, 0]),
-            ("late_half", (LONG_WAY + 1) * PIECE, half, run_of_half_patch[:]),
-        ):
-            sum_runs(name, lo, hi)
-            columns = slice(lo // PLACES - late, hi // PLACES - late)
-            nc.tensor.matmul(sums_late[:, columns], lhsT=run_sums[name][:], rhs=selector, start=True, stop=True)
+        def sum_late(lo, hi, selector):
+            sum_runs(lo, lo, hi)
+            sums = psum.tile([SAMPLES, (hi - lo) // PLACES], F32, name="sums_late")
+            nc.tensor.matmul(sums[:], lhsT=run_sums[lo][:], rhs=selector, start=True, stop=True)
+            return sums
 
-        sums_own = held.tile([SAMPLES, PATCHES - own], F32, name="sums_own")
-        by_patch = product[:, half:].rearrange("c (q i) -> c q i", i=PLACES)
-        nc.vector.tensor_reduce(sums_own[:], by_patch, AXIS.X, ALU.add)
-        v_late = held.tile([SAMPLES, own - late], F32, name="v_late")
-        nc.vector.tensor_tensor(v_late[:], sums_late[:], bias[:, late:own], ALU.add)
-        v_own = held.tile([SAMPLES, PATCHES - own], F32, name="v_own")
-        nc.vector.tensor_tensor(v_own[:], sums_own[:], bias[:, own:], ALU.add)
-        active_late = held.tile([SAMPLES, (own - late) // PER_STEP, 1, PER_STEP], F32, name="active_late")
-        nc.vector.scalar_tensor_tensor(
-            active_late[:].rearrange("c s r p -> c (s r p)"), v_late[:], SLOPE, v_late[:], ALU.mult, ALU.max
-        )
-        stretched_late = held.tile([SAMPLES, (own - late) // PER_STEP, STRETCH, PER_STEP], F32, name="stretched_late")
-        nc.scalar.activation(stretched_late[:], active_late[:].broadcast_to(stretched_late.shape), FUNC.Copy)
-        store(late, stretched_late[:])
-        stretched_own = held.tile([SAMPLES, (PATCHES - own) // PER_STEP, STRETCH, PER_STEP], F32, name="stretched_own")
-        for s in range((PATCHES - own) // PER_STEP):
-            repeated = (
-                v_own[:, s * PER_STEP : (s + 1) * PER_STEP].unsqueeze(1).broadcast_to([SAMPLES, STRETCH, PER_STEP])
+        def finish_late(lo, sums):
+            first = lo // PLACES
+            patches = sums.shape[1]
+            v = held.tile([SAMPLES, patches], F32, name=f"v{first}")
+            nc.vector.tensor_tensor(v[:], sums[:], bias[:, first : first + patches], ALU.add)
+            active = held.tile([SAMPLES, patches // PER_STEP, 1, PER_STEP], F32, name=f"active{first}")
+            nc.vector.scalar_tensor_tensor(
+                active[:].rearrange("c s r p -> c (s r p)"), v[:], SLOPE, v[:], ALU.mult, ALU.max
             )
-            nc.vector.scalar_tensor_tensor(stretched_own[:, s], repeated, SLOPE, repeated, ALU.mult, ALU.max)
-        store(own, stretched_own[:])
+            stretched = held.tile([SAMPLES, patches // PER_STEP, STRETCH, PER_STEP], F32, name=f"stretched_at{first}")
+            nc.scalar.activation(stretched[:], active[:].broadcast_to(stretched.shape), FUNC.Copy)
+            store(first, stretched[:])
+
+        late = LONG_WAY * PIECE
+        half = late + PIECE
+        own = half + HALF
+        sums_late = sum_late(late, half, run_of_patch[:, 0])
+        sums_half = sum_late(half, own, run_of_half_patch[:])
+        finish_late(late, sums_late)
+
+        first_own = own // PLACES
+        patches = (PATCHES - first_own) // 2
+        quarters = (slice(0, patches), slice(patches, 2 * patches))
+        sums_own = held.tile([SAMPLES, 2 * patches], F32, name="sums_own")
+        by_patch = product[:, own:].rearrange("c (q i) -> c q i", i=PLACES)
+        for quarter in quarters:
+            nc.vector.tensor_reduce(sums_own[:, quarter], by_patch[:, quarter], AXIS.X, ALU.add)
+        v_own = held.tile([SAMPLES, 2 * patches], F32, name="v_own")
+        bias_own = bias[:, first_own:]
+        for quarter in quarters:
+            nc.vector.tensor_tensor(v_own[:, quarter], sums_own[:, quarter], bias_own[:, quarter], ALU.add)
+        finish_late(half, sums_half)
+        stretched_own = held.tile([SAMPLES, 2, STRETCH, PER_STEP], F32, name="stretched_own")
+        for step, quarter in enumerate(quarters):
+            repeated = v_own[:, quarter].unsqueeze(1).broadcast_to([SAMPLES, STRETCH, PER_STEP])
+            nc.vector.scalar_tensor_tensor(stretched_own[:, step], repeated, SLOPE, repeated, ALU.mult, ALU.max)
+        store(first_own, stretched_own[:])

import concourse.mybir as mybir
from concourse.masks import make_identity

F32 = mybir.dt.float32
U16 = mybir.dt.uint16
ALU = mybir.AluOpType
AXIS = mybir.AxisListType
FUNC = mybir.ActivationFunctionType

SAMPLES = 128
POINTS = 2048
ENTRIES = 8192
PLACES = 32
PATCHES = ENTRIES // PLACES
PER_STEP = 8
STRETCH = 8
SLOPE = 0.3

LOOKUP_BOUNDS = (0, 1024, 2048, 3072, 4096, 5120, 6144, 7168, 7680, 7936, 8192)
LOOKUPS = tuple(zip(LOOKUP_BOUNDS[:-1], LOOKUP_BOUNDS[1:]))

PIECE = 1024
PIECES = ENTRIES // PIECE
HALF = PIECE // 2
LONG_WAY = 6

LOAD = 2048

RUNS = 128
RUN = PIECE // RUNS
PATCH_RUNS = PLACES // RUN
GROUP = PIECE // PLACES
GROUPS = 128 // GROUP

FLOPS = 2 * SAMPLES * ENTRIES


def tile_patchy_layer_returnfullseq_kernel(tc, x, w, b, offs, out):
    nc = tc.nc
    with (
        tc.tile_pool(name="held", bufs=1) as held,
        tc.psum_pool(name="psum", bufs=2) as psum,
    ):
        offsets = held.tile([SAMPLES, ENTRIES // 16], U16, name="offsets")
        nc.sync.dma_start(offsets[:], offs)
        window = held.tile([SAMPLES, POINTS], F32, name="window")
        nc.sync.dma_start(window[:], x)
        weights = held.tile([SAMPLES, ENTRIES], F32, name="weights")
        bias = held.tile([SAMPLES, PATCHES], F32, name="bias")
        for lo in range(0, ENTRIES, LOAD):
            hi = lo + LOAD
            nc.sync.dma_start(weights[:, lo:hi], w[:, lo:hi].broadcast_to([SAMPLES, hi - lo]))
            if lo == 0:
                nc.sync.dma_start(bias[:], b.broadcast_to([SAMPLES, PATCHES]))

        identity = held.tile([SAMPLES, SAMPLES], F32, name="identity")
        make_identity(nc, identity[:])

        slope_sign = held.tile([128, 1], F32, name="slope_sign")
        nc.vector.memset(slope_sign[:], 1.0)
        nc.vector.memset(slope_sign[GROUP : 2 * GROUP], -SLOPE)
        unstack = held.tile([128, GROUP], F32, name="unstack")
        nc.vector.memset(unstack[:], 0.0)
        for group, sign in ((0, 1.0), (1, -1.0)):
            nc.gpsimd.affine_select(
                out=unstack[:],
                in_=unstack[:],
                pattern=[[-1, GROUP]],
                compare_op=ALU.not_equal,
                fill=sign,
                base=-GROUP * group,
                channel_multiplier=1,
            )
        run_of_patch = held.tile([RUNS, GROUPS, GROUP], F32, name="run_of_patch")
        nc.vector.memset(run_of_patch[:], 1.0)
        nc.gpsimd.affine_select(
            out=run_of_patch[:],
            in_=run_of_patch[:],
            pattern=[[0, GROUPS], [-PATCH_RUNS, GROUP]],
            compare_op=ALU.is_ge,
            fill=0.0,
            base=0,
            channel_multiplier=1,
        )
        nc.gpsimd.affine_select(
            out=run_of_patch[:],
            in_=run_of_patch[:],
            pattern=[[0, GROUPS], [PATCH_RUNS, GROUP]],
            compare_op=ALU.is_ge,
            fill=0.0,
            base=PATCH_RUNS - 1,
            channel_multiplier=-1,
        )

        run_of_half_patch = held.tile([RUNS, GROUP // 2], F32, name="run_of_half_patch")
        by_pair = run_of_patch[:, 0].rearrange("m (q h) -> m q h", h=2)
        nc.vector.tensor_tensor(run_of_half_patch[:], by_pair[:, :, 0], by_pair[:, :, 1], ALU.add)

        bias_groups = held.tile([SAMPLES, PIECES, GROUPS, GROUP], F32, name="bias_groups")
        nc.scalar.activation(
            bias_groups[:],
            bias[:].rearrange("c (k g q) -> c k g q", g=1, q=GROUP).broadcast_to(bias_groups.shape),
            FUNC.Copy,
        )

        product = held.tile([SAMPLES, ENTRIES], F32, name="product")
        run_sums = {}
        terms = {}

        def look_up(lo, hi):
            picked = window[:].indirect(offsets[:, lo // 16 : hi // 16])
            nc.vector.tensor_tensor(product[:, lo:hi], picked, weights[:, lo:hi], ALU.mult)

        def store(first, stretched):
            columns = stretched.shape[1] * STRETCH * PER_STEP
            nc.sync.dma_start(
                out[:, first * STRETCH : first * STRETCH + columns], stretched.rearrange("c s r p -> c (s r p)")
            )

        def sum_runs(k, lo, hi):
            run = (hi - lo) // RUNS
            by_run = product[:, lo:hi].rearrange("c (m j) -> c m j", j=run)
            run_sums_psum = psum.tile([RUNS, SAMPLES], F32, name="run_sums_psum")
            for j in range(run):
                nc.tensor.matmul(
                    run_sums_psum[:],
                    lhsT=by_run[:, :, j],
                    rhs=identity[:],
                    start=(j == 0),
                    stop=(j == run - 1),
                    is_transpose=True,
                )
            run_sums[k] = held.tile([RUNS, SAMPLES], F32, name=f"run_sums{k}")
            nc.scalar.activation(run_sums[k][:], run_sums_psum[:], FUNC.Copy)

        def take_terms(k):
            v_psum = psum.tile([128, SAMPLES], F32, name="v_psum")
            nc.tensor.matmul(
                v_psum[:],
                lhsT=bias_groups[:, k].rearrange("c g q -> c (g q)"),
                rhs=identity[:],
                start=True,
                stop=False,
            )
            nc.tensor.matmul(
                v_psum[:],
                lhsT=run_of_patch[:].rearrange("m g q -> m (g q)"),
                rhs=run_sums[k][:],
                start=False,
                stop=True,
            )
            terms[k] = held.tile([128, SAMPLES], F32, name=f"terms{k}")
            nc.scalar.activation(terms[k][:], v_psum[:], FUNC.Relu, scale=slope_sign[:, 0:1])

        def stretch_and_store(k):
            active = psum.tile([SAMPLES, GROUP // PER_STEP, 1, PER_STEP], F32, name="active")
            nc.tensor.matmul(
                active[:].rearrange("c s r p -> c (s r p)"), lhsT=terms[k][:], rhs=unstack[:], start=True, stop=True
            )
            stretched = held.tile([SAMPLES, GROUP // PER_STEP, STRETCH, PER_STEP], F32, name=f"stretched{k}")
            nc.scalar.activation(stretched[:], active[:].broadcast_to(stretched.shape), FUNC.Copy)
            store(k * GROUP, stretched[:])

        for lo, hi in LOOKUPS:
            look_up(lo, hi)
            for k in range(LONG_WAY):
                if lo < (k + 1) * PIECE <= hi:
                    sum_runs(k, k * PIECE, (k + 1) * PIECE)
                    if k >= 1:
                        stretch_and_store(k - 1)
                    take_terms(k)
        stretch_and_store(LONG_WAY - 1)

        def sum_late(lo, hi, selector):
            sum_runs(lo, lo, hi)
            sums = psum.tile([SAMPLES, (hi - lo) // PLACES], F32, name="sums_late")
            nc.tensor.matmul(sums[:], lhsT=run_sums[lo][:], rhs=selector, start=True, stop=True)
            return sums

        def finish_late(lo, sums):
            first = lo // PLACES
            patches = sums.shape[1]
            v = held.tile([SAMPLES, patches], F32, name=f"v{first}")
            nc.vector.tensor_tensor(v[:], sums[:], bias[:, first : first + patches], ALU.add)
            active = held.tile([SAMPLES, patches // PER_STEP, 1, PER_STEP], F32, name=f"active{first}")
            nc.vector.scalar_tensor_tensor(
                active[:].rearrange("c s r p -> c (s r p)"), v[:], SLOPE, v[:], ALU.mult, ALU.max
            )
            stretched = held.tile([SAMPLES, patches // PER_STEP, STRETCH, PER_STEP], F32, name=f"stretched_at{first}")
            nc.scalar.activation(stretched[:], active[:].broadcast_to(stretched.shape), FUNC.Copy)
            store(first, stretched[:])

        late = LONG_WAY * PIECE
        half = late + PIECE
        own = half + HALF
        sums_late = sum_late(late, half, run_of_patch[:, 0])
        sums_half = sum_late(half, own, run_of_half_patch[:])
        finish_late(late, sums_late)

        first_own = own // PLACES
        patches = (PATCHES - first_own) // 2
        quarters = (slice(0, patches), slice(patches, 2 * patches))
        sums_own = held.tile([SAMPLES, 2 * patches], F32, name="sums_own")
        by_patch = product[:, own:].rearrange("c (q i) -> c q i", i=PLACES)
        for quarter in quarters:
            nc.vector.tensor_reduce(sums_own[:, quarter], by_patch[:, quarter], AXIS.X, ALU.add)
        v_own = held.tile([SAMPLES, 2 * patches], F32, name="v_own")
        bias_own = bias[:, first_own:]
        for quarter in quarters:
            nc.vector.tensor_tensor(v_own[:, quarter], sums_own[:, quarter], bias_own[:, quarter], ALU.add)
        finish_late(half, sums_half)
        stretched_own = held.tile([SAMPLES, 2, STRETCH, PER_STEP], F32, name="stretched_own")
        for step, quarter in enumerate(quarters):
            repeated = v_own[:, quarter].unsqueeze(1).broadcast_to([SAMPLES, STRETCH, PER_STEP])
            nc.vector.scalar_tensor_tensor(stretched_own[:, step], repeated, SLOPE, repeated, ALU.mult, ALU.max)
        store(first_own, stretched_own[:])
